import numpy as np
import ml_dtypes


def mxq(x, axis, fmt="e4m3"):
    dtype, down = {"e4m3": (ml_dtypes.float8_e4m3fn, 7), "e5m2": (ml_dtypes.float8_e5m2, 14)}[fmt]
    v = np.moveaxis(np.asarray(x, np.float32).astype(ml_dtypes.bfloat16).astype(np.float64), axis, -1)
    blocks = v.reshape(v.shape[:-1] + (-1, 32))
    amax = np.abs(blocks).max(-1, keepdims=True)
    byte = np.maximum(np.where(amax > 0, np.frexp(amax)[1] - 1 + 127, 0) - down, 1)
    scale = np.exp2(byte - 127.0)
    codes = (blocks / scale).astype(np.float32).astype(dtype).astype(np.float64)
    return np.moveaxis((codes * scale).reshape(v.shape), -1, axis)


WIDE = False


def mx_kscale(k):
    if not WIDE:
        return np.ones(k)
    levels = np.array([10, -10, 5, -5, 0])
    if k % 512:
        return np.exp2(np.random.permutation(np.resize(levels, k // 32))).repeat(32)
    a = np.empty((k // 512, 16))
    for p in range(k // 512):
        a[p, :8] = np.random.permutation(np.resize(levels, 8))
        for g in range(8):
            far = levels[np.abs(levels - a[p, g]) >= 10]
            a[p, g + 8] = far[np.random.randint(len(far))]
    return np.exp2(a.ravel()).repeat(32)


BF16 = ml_dtypes.bfloat16


def bf(x):
    return np.asarray(x, np.float32).astype(BF16)


def f64(x):
    return np.asarray(x).astype(np.float64)


M, K, P, Q = 256, 2048, 128, 16
N = P * Q
SCALING = 2.0


def _kron(A, B):
    m, n = A.shape
    p, q = B.shape
    return (A[:, None, :, None] * B[None, :, None, :]).reshape(m * p, n * q)


def setup_inputs():
    s = mx_kscale(K)
    return {"x": bf(np.random.standard_normal((M, K)) * s),
            "original_weight": bf(np.random.standard_normal((N, K)) / np.sqrt(K) / s),
            "lokr_A": bf(np.random.standard_normal((P, K)) / np.sqrt(K) / s),
            "lokr_B": bf(np.random.standard_normal((Q, 1)) * 0.25),
            "scalar": bf(1.5 + 0.1 * np.random.standard_normal(1))}


def reference(x, original_weight, lokr_A, lokr_B, scalar):
    delta_W = _kron(f64(lokr_A), f64(lokr_B)) * SCALING
    W_eff = f64(original_weight) + f64(scalar)[0] * delta_W
    return mxq(f64(x), 1, "e4m3") @ mxq(W_eff, 1, "e4m3").T

@@ -1,0 +1,240 @@
+from contextlib import ExitStack
+
+import concourse.mybir as mybir
+from concourse.masks import make_identity
+
+FP8X4 = mybir.dt.float8_e4m3fn_x4
+BF16 = mybir.dt.bfloat16
+F32 = mybir.dt.float32
+U32 = mybir.dt.uint32
+U8 = mybir.dt.uint8
+ALU = mybir.AluOpType
+ACT = mybir.ActivationFunctionType
+
+FLOPS = 2 * 256 * 2048 * 2048
+
+P = 128
+NG = 4
+NQ = 16
+CHUNK = 8
+
+V_QS = [0, 2, 3, 6, 7, 8, 10, 11, 13, 15]
+G_QS = [1, 4, 9, 12, 14]
+T_Q = 5
+LOADS = [0, 1, 2, 5, 3, 4, 6, 7, 8, 9, "x", 10, 11, 12, 13, 14, 15]
+
+
+def tile_lokrlayer_kernel(tc, x, original_weight, lokr_A, lokr_B, scalar, out):
+    nc = tc.nc
+    with ExitStack() as ctx:
+        const = ctx.enter_context(tc.tile_pool(name="const", bufs=1))
+        spool = ctx.enter_context(tc.tile_pool(name="spool", bufs=1))
+        vps = ctx.enter_context(tc.psum_pool(name="vps", bufs=4))
+        sps = ctx.enter_context(tc.psum_pool(name="sps", bufs=4))
+        ctx.enter_context(tc.manual_schedule())
+
+        ident = const.tile([P, P], F32, name="ident")
+        make_identity(nc, ident[:])
+
+        b_bc = const.tile([P, NQ], BF16, name="b_bc")
+        nc.scalar.dma_start(out=b_bc[:], in_=lokr_B.rearrange("q o -> (q o)").partition_broadcast(P))
+        s_bc = const.tile([P, 1], BF16, name="s_bc")
+        nc.scalar.dma_start(out=s_bc[:], in_=scalar.partition_broadcast(P))
+        a_sb = const.tile([P, 2048], BF16, name="a_sb")
+        for b in range(2):
+            nc.sync.dma_start(out=a_sb[:, b * 1024:(b + 1) * 1024], in_=lokr_A[:, b * 1024:(b + 1) * 1024])
+        w_rows = original_weight.rearrange("(p q) k -> q p k", q=NQ)
+        w_sb = {}
+        x_sb = const.tile([P, 2, 2048], BF16, name="x_sb")
+        for q in LOADS:
+            if q == "x":
+                nc.sync.dma_start(out=x_sb[:], in_=x.rearrange("(t m) k -> m t k", t=2))
+            else:
+                w_sb[q] = const.tile([P, 2048], BF16, name="w%d" % q)
+                nc.sync.dma_start(out=w_sb[q][:], in_=w_rows[q])
+
+        s32 = const.tile([P, 1], F32, name="s32")
+        nc.vector.tensor_copy(out=s32[:], in_=s_bc[:])
+        gain = const.tile([P, NQ], F32, name="gain")
+        nc.vector.tensor_scalar(
+            out=gain[:], in0=b_bc[:], scalar1=s32[:, 0:1], scalar2=2.0, op0=ALU.mult, op1=ALU.mult
+        )
+
+        def transpose_words(bank, words, b):
+            for g2 in range(2):
+                for u in range(2):
+                    w0 = 256 * (2 * b + g2)
+                    nc.tensor.transpose(
+                        out=bank[:, g2 * 256 + u:(g2 + 1) * 256:2],
+                        in_=words[:, w0 + u:w0 + 256:2],
+                        identity=ident[:],
+                    )
+
+        grouped = const.tile([P, NG, 2, NQ, 256], BF16, name="grouped", align_bytes=64)
+        grouped_words = grouped[:].rearrange("p g h q j -> p (g h q j)").bitcast(F32).rearrange(
+            "p (a q j) -> p a q j", a=2 * NG, q=NQ
+        )
+
+        def grouped_slice(q, b):
+            return grouped[:].rearrange("p g h q j -> p (g h) q j")[:, 4 * b:4 * (b + 1), q, :]
+
+        at = const.tile([P, 2048], BF16, name="at")
+
+        def delta_add(j):
+            q, b = G_QS[j // 2], j % 2
+            cols = slice(b * 1024, (b + 1) * 1024)
+            delta = spool.tile([P, 2, 256, 2], F32, name="delta%d" % j, tag="delta", bufs=3)
+            nc.scalar.activation(
+                out=delta[:],
+                in_=a_sb[:, cols].rearrange("p (w u e) -> p u w e", u=2, e=2),
+                func=ACT.Copy,
+                scale=gain[:, q:q + 1],
+            )
+            wn = spool.tile([P, 2, 256, 2], BF16, name="wn%d" % j, tag="wn", bufs=4)
+            nc.gpsimd.tensor_tensor(
+                out=wn[:],
+                in0=w_sb[q][:, cols].rearrange("p (w u e) -> p u w e", u=2, e=2),
+                in1=delta[:],
+                op=ALU.add,
+            )
+            return wn
+
+        def flush(j, wn):
+            q, b = G_QS[j // 2], j % 2
+            bank = sps.tile([P, 512], F32, name="ps%d" % j, tag="s")
+            words = wn[:].rearrange("p u w e -> p (u w e)").bitcast(F32)
+            for g2 in range(2):
+                for u in range(2):
+                    w0 = u * 256 + g2 * P
+                    nc.tensor.transpose(
+                        out=bank[:, g2 * 256 + u:(g2 + 1) * 256:2], in_=words[:, w0:w0 + P], identity=ident[:]
+                    )
+            nc.scalar.copy(
+                out=grouped_words[:, 4 * b:4 * (b + 1), q, :],
+                in_=bank[:].rearrange("p (a j) -> p a j", a=4),
+            )
+
+        for b in range(2):
+            pa = sps.tile([P, 512], F32, name="pa%d" % b, tag="s")
+            transpose_words(pa, a_sb[:].bitcast(F32), b)
+            dst = at[:].bitcast(F32)[:, b * 512:(b + 1) * 512]
+            if b == 0:
+                nc.vector.tensor_copy(out=dst, in_=pa[:])
+            else:
+                nc.scalar.copy(out=dst, in_=pa[:])
+
+        ident_bf = const.tile([P, P], BF16, name="ident_bf")
+        hi = const.tile([P, P], BF16, name="hi")
+        lo = const.tile([P, P], BF16, name="lo")
+        g_hi = const.tile([P, 1], BF16, name="g_hi")
+        g_lo = const.tile([P, 1], F32, name="g_lo")
+
+        def make_diagonals():
+            nc.gpsimd.tensor_copy(out=ident_bf[:], in_=ident[:])
+            nc.vector.tensor_copy(out=g_hi[:], in_=gain[:, T_Q:T_Q + 1])
+            nc.vector.tensor_tensor(out=g_lo[:], in0=gain[:, T_Q:T_Q + 1], in1=g_hi[:], op=ALU.subtract)
+            nc.vector.tensor_scalar(out=hi[:], in0=ident[:], scalar1=gain[:, T_Q:T_Q + 1], scalar2=None, op0=ALU.mult)
+            nc.vector.tensor_scalar(out=lo[:], in0=ident[:], scalar1=g_lo[:, 0:1], scalar2=None, op0=ALU.mult)
+
+        def tensor_pass(g):
+            bank = sps.tile([P, 4, P], F32, name="pt%d" % g, tag="s")
+            for t in range(4):
+                cols = slice(512 * g + t, 512 * (g + 1), 4)
+                nc.tensor.matmul(out=bank[:, t, :], lhsT=w_sb[T_Q][:, cols], rhs=ident_bf[:], start=True, stop=False)
+                nc.tensor.matmul(out=bank[:, t, :], lhsT=a_sb[:, cols], rhs=hi[:], start=False, stop=False)
+                nc.tensor.matmul(out=bank[:, t, :], lhsT=a_sb[:, cols], rhs=lo[:], start=False, stop=True)
+            for h in range(2):
+                nc.scalar.copy(
+                    out=grouped[:, g, h, T_Q, :].rearrange("p (r t) -> p r t", t=4),
+                    in_=bank[:, :, h * 64:(h + 1) * 64].rearrange("p t r -> p r t"),
+                )
+
+        xg = const.tile([P, 4096], BF16, name="xg", align_bytes=64)
+        x_codes = const.tile([P, 1024], U32, name="x_codes", align_bytes=64)
+        x_scales = const.tile([P, 1024], U8, name="x_scales", align_bytes=64)
+
+        def x_pass(g):
+            px = sps.tile([P, 512], F32, name="px%d" % g, tag="s")
+            for t in range(2):
+                for u in range(2):
+                    nc.tensor.transpose(
+                        out=px[:, t * 256 + u:(t + 1) * 256:2],
+                        in_=x_sb[:, t, :].bitcast(F32)[:, 256 * g + u:256 * (g + 1):2],
+                        identity=ident[:],
+                    )
+            nc.scalar.copy(out=xg[:].bitcast(F32)[:, g * 512:(g + 1) * 512], in_=px[:])
+
+        sums = {}
+        extras = {}
+        for g in range(NG):
+            extras[5 + 2 * g] = (tensor_pass, g)
+            extras[13 + 2 * g] = (x_pass, g)
+        for i in range(2 * len(V_QS)):
+            q, b = V_QS[i // 2], i % 2
+            if i % 2 == 0:
+                sums[i // 2] = delta_add(i // 2)
+            if i == 0:
+                make_diagonals()
+            bank = vps.tile([P, 512], F32, name="pv%d" % i, tag="v")
+            transpose_words(bank, w_sb[q][:].bitcast(F32), b)
+            nc.vector.scalar_tensor_tensor(
+                out=grouped_slice(q, b),
+                in0=at[:, b * 1024:(b + 1) * 1024].rearrange("p (a j) -> p a j", a=4),
+                scalar=gain[:, q:q + 1],
+                in1=bank[:].bitcast(BF16).rearrange("p (a j) -> p a j", a=4),
+                op0=ALU.mult,
+                op1=ALU.add,
+            )
+            if i >= 6 and i % 2 == 0:
+                flush((i - 6) // 2, sums[(i - 6) // 2])
+            if i in extras:
+                extras[i][0](extras[i][1])
+        for j in range(7, 10):
+            flush(j, sums[j])
+
+        codes = const.tile([P, 4, NG, CHUNK * 64], U32, name="codes", align_bytes=64)
+        scales = const.tile([P, 4, NG, CHUNK * 64], U8, name="scales", align_bytes=64)
+        out_sb = {}
+        for c in range(4):
+            h, q0 = c // 2, CHUNK * (c % 2)
+            accs = [
+                vps.tile([P, CHUNK * 64], F32, name="acc%d_0" % c, tag="v"),
+                sps.tile([P, CHUNK * 64], F32, name="acc%d_1" % c, tag="s"),
+            ]
+            for g in range(NG):
+                if c == 0:
+                    nc.vector.quantize_mx(
+                        out=x_codes[:, g * 256:(g + 1) * 256].bitcast(FP8X4),
+                        scales=x_scales[:, g * 256:(g + 1) * 256],
+                        in_=xg[:, g * 1024:(g + 1) * 1024],
+                    )
+                nc.vector.quantize_mx(
+                    out=codes[:, c, g, :].bitcast(FP8X4),
+                    scales=scales[:, c, g, :],
+                    in_=grouped[:, g, h, q0:q0 + CHUNK, :].rearrange("p q j -> p (q j)"),
+                )
+                for t in range(2):
+                    m0 = g * 256 + t * P
+                    nc.tensor.matmul_mx(
+                        out=accs[t][:],
+                        lhsT=x_codes[:, m0:m0 + P].bitcast(FP8X4),
+                        lhsT_scale=x_scales[:, m0:m0 + P],
+                        rhs=codes[:, c, g, :].bitcast(FP8X4),
+                        rhs_scale=scales[:, c, g, :],
+                        start=(g == 0),
+                        stop=(g == NG - 1),
+                    )
+            for t in range(2):
+                if q0 == 0:
+                    out_sb[(h, t)] = const.tile([P, 64, NQ], F32, name="out_sb%d%d" % (h, t))
+                dst = out_sb[(h, t)][:, :, q0:q0 + CHUNK]
+                src = accs[t][:].rearrange("m (q r) -> m r q", q=CHUNK)
+                if c == 3 and t == 1:
+                    nc.vector.tensor_copy(out=dst, in_=src)
+                else:
+                    nc.scalar.copy(out=dst, in_=src)
+                if q0 + CHUNK == NQ:
+                    nc.sync.dma_start(
+                        out=out[t * P:(t + 1) * P, h * 1024:(h + 1) * 1024],
+                        in_=out_sb[(h, t)][:].rearrange("m r q -> m (r q)"),
+                    )

@@ -18,10 +18,10 @@ NG = 4
 NQ = 16
 CHUNK = 8
 
-V_QS = [0, 2, 3, 6, 7, 8, 10, 11, 13, 15]
-G_QS = [1, 4, 9, 12, 14]
-T_Q = 5
-LOADS = [0, 1, 2, 5, 3, 4, 6, 7, 8, 9, "x", 10, 11, 12, 13, 14, 15]
+V_QS = [0, 1, 8, 9, 10, 11, 12, 13, 14, 15]
+G_QS = [2, 3, 4, 5, 6]
+T_Q = 7
+LOADS = [0, 2, 1, 7, 8, 3, 9, 10, 4, 11, "x", 12, 5, 13, 14, 6, 15]
 
 
 def tile_lokrlayer_kernel(tc, x, original_weight, lokr_A, lokr_B, scalar, out):
@@ -70,13 +70,17 @@ def tile_lokrlayer_kernel(tc, x, original_weight, lokr_A, lokr_B, scalar, out):
                         identity=ident[:],
                     )
 
-        grouped = const.tile([P, NG, 2, NQ, 256], BF16, name="grouped", align_bytes=64)
-        grouped_words = grouped[:].rearrange("p g h q j -> p (g h q j)").bitcast(F32).rearrange(
-            "p (a q j) -> p a q j", a=2 * NG, q=NQ
+        grouped = [
+            const.tile([P, NG, 2, CHUNK, 256], BF16, name="grouped0", align_bytes=64),
+            const.tile([P, NG, 2, CHUNK, 256], BF16, name="grouped1", align_bytes=64),
+        ]
+        grouped_words = grouped[0][:].rearrange("p g h q j -> p (g h q j)").bitcast(F32).rearrange(
+            "p (a q j) -> p a q j", a=2 * NG, q=CHUNK
         )
 
         def grouped_slice(q, b):
-            return grouped[:].rearrange("p g h q j -> p (g h) q j")[:, 4 * b:4 * (b + 1), q, :]
+            tile = grouped[q // CHUNK]
+            return tile[:].rearrange("p g h q j -> p (g h) q j")[:, 4 * b:4 * (b + 1), q % CHUNK, :]
 
         at = const.tile([P, 2048], BF16, name="at")
 
@@ -145,7 +149,7 @@ def tile_lokrlayer_kernel(tc, x, original_weight, lokr_A, lokr_B, scalar, out):
                 nc.tensor.matmul(out=bank[:, t, :], lhsT=a_sb[:, cols], rhs=lo[:], start=False, stop=True)
             for h in range(2):
                 nc.scalar.copy(
-                    out=grouped[:, g, h, T_Q, :].rearrange("p (r t) -> p r t", t=4),
+                    out=grouped[0][:, g, h, T_Q, :].rearrange("p (r t) -> p r t", t=4),
                     in_=bank[:, :, h * 64:(h + 1) * 64].rearrange("p t r -> p r t"),
                 )
 
@@ -189,14 +193,13 @@ def tile_lokrlayer_kernel(tc, x, original_weight, lokr_A, lokr_B, scalar, out):
                 flush((i - 6) // 2, sums[(i - 6) // 2])
             if i in extras:
                 extras[i][0](extras[i][1])
-        for j in range(7, 10):
-            flush(j, sums[j])
+        flush(7, sums[7])
 
         codes = const.tile([P, 4, NG, CHUNK * 64], U32, name="codes", align_bytes=64)
         scales = const.tile([P, 4, NG, CHUNK * 64], U8, name="scales", align_bytes=64)
         out_sb = {}
         for c in range(4):
-            h, q0 = c // 2, CHUNK * (c % 2)
+            h, q0 = c // 2, CHUNK * (1 - c % 2)
             accs = [
                 vps.tile([P, CHUNK * 64], F32, name="acc%d_0" % c, tag="v"),
                 sps.tile([P, CHUNK * 64], F32, name="acc%d_1" % c, tag="s"),
@@ -211,7 +214,7 @@ def tile_lokrlayer_kernel(tc, x, original_weight, lokr_A, lokr_B, scalar, out):
                 nc.vector.quantize_mx(
                     out=codes[:, c, g, :].bitcast(FP8X4),
                     scales=scales[:, c, g, :],
-                    in_=grouped[:, g, h, q0:q0 + CHUNK, :].rearrange("p q j -> p (q j)"),
+                    in_=grouped[q0 // CHUNK][:, g, h, :, :].rearrange("p q j -> p (q j)"),
                 )
                 for t in range(2):
                     m0 = g * 256 + t * P
@@ -224,8 +227,10 @@ def tile_lokrlayer_kernel(tc, x, original_weight, lokr_A, lokr_B, scalar, out):
                         start=(g == 0),
                         stop=(g == NG - 1),
                     )
+                if c == 0 and g % 2 == 0:
+                    flush(8 + g // 2, sums[8 + g // 2])
             for t in range(2):
-                if q0 == 0:
+                if c % 2 == 0:
                     out_sb[(h, t)] = const.tile([P, 64, NQ], F32, name="out_sb%d%d" % (h, t))
                 dst = out_sb[(h, t)][:, :, q0:q0 + CHUNK]
                 src = accs[t][:].rearrange("m (q r) -> m r q", q=CHUNK)
@@ -233,7 +238,7 @@ def tile_lokrlayer_kernel(tc, x, original_weight, lokr_A, lokr_B, scalar, out):
                     nc.vector.tensor_copy(out=dst, in_=src)
                 else:
                     nc.scalar.copy(out=dst, in_=src)
-                if q0 + CHUNK == NQ:
+                if c % 2 == 1:
                     nc.sync.dma_start(
                         out=out[t * P:(t + 1) * P, h * 1024:(h + 1) * 1024],
                         in_=out_sb[(h, t)][:].rearrange("m r q -> m (r q)"),

@@ -18,10 +18,10 @@ NG = 4
 NQ = 16
 CHUNK = 8
 
-V_QS = [0, 1, 8, 9, 10, 11, 12, 13, 14, 15]
-G_QS = [2, 3, 4, 5, 6]
+V_UNITS = [(q, b) for q in (0, 1) for b in range(2)] + [(6, 0)] + [(q, b) for q in range(8, 16) for b in range(2)]
+G_UNITS = [(q, b) for q in (2, 3, 4, 5) for b in range(2)] + [(6, 1)]
 T_Q = 7
-LOADS = [0, 2, 1, 7, 8, 3, 9, 10, 4, 11, "x", 12, 5, 13, 14, 6, 15]
+LOADS = [2, 1, 6, 8, 3, 9, 7, 10, 4, 11, "x", 12, 5, 13, 14, 15]
 
 
 def tile_lokrlayer_kernel(tc, x, original_weight, lokr_A, lokr_B, scalar, out):
@@ -36,15 +36,21 @@ def tile_lokrlayer_kernel(tc, x, original_weight, lokr_A, lokr_B, scalar, out):
         ident = const.tile([P, P], F32, name="ident")
         make_identity(nc, ident[:])
 
-        b_bc = const.tile([P, NQ], BF16, name="b_bc")
-        nc.scalar.dma_start(out=b_bc[:], in_=lokr_B.rearrange("q o -> (q o)").partition_broadcast(P))
-        s_bc = const.tile([P, 1], BF16, name="s_bc")
-        nc.scalar.dma_start(out=s_bc[:], in_=scalar.partition_broadcast(P))
+        small = const.tile([P, 2 * NQ], BF16, name="small")
+        nc.vector.memset(small[:], 0.0)
+        ones = const.tile([P, P], BF16, name="ones")
+        nc.vector.memset(ones[:], 1.0)
+        nc.sync.dma_start(out=small[0:1, 0:NQ], in_=lokr_B.rearrange("q o -> o q"))
+        nc.sync.dma_start(out=small[0:1, NQ:NQ + 1], in_=scalar.unsqueeze(0))
+        warm = const.tile([P, 1], F32, name="warm")
+        nc.scalar.copy(out=warm[:], in_=ones[:, 0:1])
         a_sb = const.tile([P, 2048], BF16, name="a_sb")
-        for b in range(2):
-            nc.sync.dma_start(out=a_sb[:, b * 1024:(b + 1) * 1024], in_=lokr_A[:, b * 1024:(b + 1) * 1024])
         w_rows = original_weight.rearrange("(p q) k -> q p k", q=NQ)
-        w_sb = {}
+        w_sb = {0: const.tile([P, 2048], BF16, name="w0")}
+        for b in range(2):
+            cols = slice(b * 1024, (b + 1) * 1024)
+            nc.sync.dma_start(out=a_sb[:, cols], in_=lokr_A[:, cols])
+            nc.sync.dma_start(out=w_sb[0][:, cols], in_=w_rows[0][:, cols])
         x_sb = const.tile([P, 2, 2048], BF16, name="x_sb")
         for q in LOADS:
             if q == "x":
@@ -53,12 +59,14 @@ def tile_lokrlayer_kernel(tc, x, original_weight, lokr_A, lokr_B, scalar, out):
                 w_sb[q] = const.tile([P, 2048], BF16, name="w%d" % q)
                 nc.sync.dma_start(out=w_sb[q][:], in_=w_rows[q])
 
-        s32 = const.tile([P, 1], F32, name="s32")
-        nc.vector.tensor_copy(out=s32[:], in_=s_bc[:])
         gain = const.tile([P, NQ], F32, name="gain")
-        nc.vector.tensor_scalar(
-            out=gain[:], in0=b_bc[:], scalar1=s32[:, 0:1], scalar2=2.0, op0=ALU.mult, op1=ALU.mult
-        )
+
+        def make_gain():
+            spread = vps.tile([P, 2 * NQ], F32, name="spread", tag="v")
+            nc.tensor.matmul(out=spread[:], lhsT=ones[:], rhs=small[:], start=True, stop=True)
+            nc.vector.tensor_scalar(
+                out=gain[:], in0=spread[:, 0:NQ], scalar1=spread[:, NQ:NQ + 1], scalar2=2.0, op0=ALU.mult, op1=ALU.mult
+            )
 
         def transpose_words(bank, words, b):
             for g2 in range(2):
@@ -71,21 +79,21 @@ def tile_lokrlayer_kernel(tc, x, original_weight, lokr_A, lokr_B, scalar, out):
                     )
 
         grouped = [
-            const.tile([P, NG, 2, CHUNK, 256], BF16, name="grouped0", align_bytes=64),
-            const.tile([P, NG, 2, CHUNK, 256], BF16, name="grouped1", align_bytes=64),
+            const.tile([P, NG, 4, CHUNK, 128], BF16, name="grouped0", align_bytes=64),
+            const.tile([P, NG, 4, CHUNK, 128], BF16, name="grouped1", align_bytes=64),
         ]
         grouped_words = grouped[0][:].rearrange("p g h q j -> p (g h q j)").bitcast(F32).rearrange(
-            "p (a q j) -> p a q j", a=2 * NG, q=CHUNK
+            "p (a q j) -> p a q j", a=4 * NG, q=CHUNK
         )
 
         def grouped_slice(q, b):
             tile = grouped[q // CHUNK]
-            return tile[:].rearrange("p g h q j -> p (g h) q j")[:, 4 * b:4 * (b + 1), q % CHUNK, :]
+            return tile[:].rearrange("p g h q j -> p (g h) q j")[:, 8 * b:8 * (b + 1), q % CHUNK, :]
 
         at = const.tile([P, 2048], BF16, name="at")
 
         def delta_add(j):
-            q, b = G_QS[j // 2], j % 2
+            q, b = G_UNITS[j]
             cols = slice(b * 1024, (b + 1) * 1024)
             delta = spool.tile([P, 2, 256, 2], F32, name="delta%d" % j, tag="delta", bufs=3)
             nc.scalar.activation(
@@ -104,7 +112,7 @@ def tile_lokrlayer_kernel(tc, x, original_weight, lokr_A, lokr_B, scalar, out):
             return wn
 
         def flush(j, wn):
-            q, b = G_QS[j // 2], j % 2
+            q, b = G_UNITS[j]
             bank = sps.tile([P, 512], F32, name="ps%d" % j, tag="s")
             words = wn[:].rearrange("p u w e -> p (u w e)").bitcast(F32)
             for g2 in range(2):
@@ -114,11 +122,11 @@ def tile_lokrlayer_kernel(tc, x, original_weight, lokr_A, lokr_B, scalar, out):
                         out=bank[:, g2 * 256 + u:(g2 + 1) * 256:2], in_=words[:, w0:w0 + P], identity=ident[:]
                     )
             nc.scalar.copy(
-                out=grouped_words[:, 4 * b:4 * (b + 1), q, :],
-                in_=bank[:].rearrange("p (a j) -> p a j", a=4),
+                out=grouped_words[:, 8 * b:8 * (b + 1), q, :],
+                in_=bank[:].rearrange("p (a j) -> p a j", a=8),
             )
 
-        for b in range(2):
+        def transpose_a(b):
             pa = sps.tile([P, 512], F32, name="pa%d" % b, tag="s")
             transpose_words(pa, a_sb[:].bitcast(F32), b)
             dst = at[:].bitcast(F32)[:, b * 512:(b + 1) * 512]
@@ -147,11 +155,10 @@ def tile_lokrlayer_kernel(tc, x, original_weight, lokr_A, lokr_B, scalar, out):
                 nc.tensor.matmul(out=bank[:, t, :], lhsT=w_sb[T_Q][:, cols], rhs=ident_bf[:], start=True, stop=False)
                 nc.tensor.matmul(out=bank[:, t, :], lhsT=a_sb[:, cols], rhs=hi[:], start=False, stop=False)
                 nc.tensor.matmul(out=bank[:, t, :], lhsT=a_sb[:, cols], rhs=lo[:], start=False, stop=True)
-            for h in range(2):
-                nc.scalar.copy(
-                    out=grouped[0][:, g, h, T_Q, :].rearrange("p (r t) -> p r t", t=4),
-                    in_=bank[:, :, h * 64:(h + 1) * 64].rearrange("p t r -> p r t"),
-                )
+            nc.scalar.copy(
+                out=grouped[0][:, g, :, T_Q, :].rearrange("p h (r t) -> p h r t", t=4),
+                in_=bank[:].rearrange("p t (h r) -> p h r t", h=4),
+            )
 
         xg = const.tile([P, 4096], BF16, name="xg", align_bytes=64)
         x_codes = const.tile([P, 1024], U32, name="x_codes", align_bytes=64)
@@ -171,21 +178,25 @@ def tile_lokrlayer_kernel(tc, x, original_weight, lokr_A, lokr_B, scalar, out):
         sums = {}
         extras = {}
         for g in range(NG):
-            extras[5 + 2 * g] = (tensor_pass, g)
-            extras[13 + 2 * g] = (x_pass, g)
-        for i in range(2 * len(V_QS)):
-            q, b = V_QS[i // 2], i % 2
-            if i % 2 == 0:
-                sums[i // 2] = delta_add(i // 2)
+            extras[11 + g] = (tensor_pass, g)
+            extras[16 + g] = (x_pass, g)
+        for i in range(len(V_UNITS)):
+            q, b = V_UNITS[i]
+            if i < 2:
+                transpose_a(i)
             if i == 0:
+                make_gain()
+            if i % 2 == 0 and i // 2 < len(G_UNITS):
+                sums[i // 2] = delta_add(i // 2)
+            if i == 2:
                 make_diagonals()
             bank = vps.tile([P, 512], F32, name="pv%d" % i, tag="v")
             transpose_words(bank, w_sb[q][:].bitcast(F32), b)
             nc.vector.scalar_tensor_tensor(
                 out=grouped_slice(q, b),
-                in0=at[:, b * 1024:(b + 1) * 1024].rearrange("p (a j) -> p a j", a=4),
+                in0=at[:, b * 1024:(b + 1) * 1024].rearrange("p (a j) -> p a j", a=8),
                 scalar=gain[:, q:q + 1],
-                in1=bank[:].bitcast(BF16).rearrange("p (a j) -> p a j", a=4),
+                in1=bank[:].bitcast(BF16).rearrange("p (a j) -> p a j", a=8),
                 op0=ALU.mult,
                 op1=ALU.add,
             )
@@ -193,16 +204,20 @@ def tile_lokrlayer_kernel(tc, x, original_weight, lokr_A, lokr_B, scalar, out):
                 flush((i - 6) // 2, sums[(i - 6) // 2])
             if i in extras:
                 extras[i][0](extras[i][1])
-        flush(7, sums[7])
+        flush(8, sums[8])
 
-        codes = const.tile([P, 4, NG, CHUNK * 64], U32, name="codes", align_bytes=64)
-        scales = const.tile([P, 4, NG, CHUNK * 64], U8, name="scales", align_bytes=64)
-        out_sb = {}
-        for c in range(4):
-            h, q0 = c // 2, CHUNK * (1 - c % 2)
+        out_sb = []
+        for n in range(4):
+            out_tile = const.tile([P, 64, NQ], F32, name="out_sb%d" % n)
+            out_sb.append(out_tile)
+        chunks = [(1, 0, 2), (0, 0, 2), (1, 2, 2), (0, 2, 1), (0, 3, 1)]
+        for c, (part, h0, count) in enumerate(chunks):
+            width = count * CHUNK * 32
+            codes = const.tile([P, NG, width], U32, name="codes%d" % c, align_bytes=64)
+            scales = const.tile([P, NG, width], U8, name="scales%d" % c, align_bytes=64)
             accs = [
-                vps.tile([P, CHUNK * 64], F32, name="acc%d_0" % c, tag="v"),
-                sps.tile([P, CHUNK * 64], F32, name="acc%d_1" % c, tag="s"),
+                vps.tile([P, width], F32, name="acc%d_0" % c, tag="v"),
+                sps.tile([P, width], F32, name="acc%d_1" % c, tag="s"),
             ]
             for g in range(NG):
                 if c == 0:
@@ -212,9 +227,9 @@ def tile_lokrlayer_kernel(tc, x, original_weight, lokr_A, lokr_B, scalar, out):
                         in_=xg[:, g * 1024:(g + 1) * 1024],
                     )
                 nc.vector.quantize_mx(
-                    out=codes[:, c, g, :].bitcast(FP8X4),
-                    scales=scales[:, c, g, :],
-                    in_=grouped[q0 // CHUNK][:, g, h, :, :].rearrange("p q j -> p (q j)"),
+                    out=codes[:, g, :].bitcast(FP8X4),
+                    scales=scales[:, g, :],
+                    in_=grouped[part][:, g, h0:h0 + count, :, :].rearrange("p h q j -> p (h q j)"),
                 )
                 for t in range(2):
                     m0 = g * 256 + t * P
@@ -222,24 +237,22 @@ def tile_lokrlayer_kernel(tc, x, original_weight, lokr_A, lokr_B, scalar, out):
                         out=accs[t][:],
                         lhsT=x_codes[:, m0:m0 + P].bitcast(FP8X4),
                         lhsT_scale=x_scales[:, m0:m0 + P],
-                        rhs=codes[:, c, g, :].bitcast(FP8X4),
-                        rhs_scale=scales[:, c, g, :],
+                        rhs=codes[:, g, :].bitcast(FP8X4),
+                        rhs_scale=scales[:, g, :],
                         start=(g == 0),
                         stop=(g == NG - 1),
                     )
-                if c == 0 and g % 2 == 0:
-                    flush(8 + g // 2, sums[8 + g // 2])
             for t in range(2):
-                if c % 2 == 0:
-                    out_sb[(h, t)] = const.tile([P, 64, NQ], F32, name="out_sb%d%d" % (h, t))
-                dst = out_sb[(h, t)][:, :, q0:q0 + CHUNK]
-                src = accs[t][:].rearrange("m (q r) -> m r q", q=CHUNK)
-                if c == 3 and t == 1:
+                rows = slice(32 * (h0 % 2), 32 * (h0 % 2 + count))
+                res = out_sb[2 * (h0 // 2) + t]
+                dst = res[:, rows, part * CHUNK:(part + 1) * CHUNK].rearrange("m (h r) q -> m h r q", h=count)
+                src = accs[t][:].rearrange("m (h q r) -> m h r q", h=count, q=CHUNK)
+                if c == len(chunks) - 1 and t == 1:
                     nc.vector.tensor_copy(out=dst, in_=src)
                 else:
                     nc.scalar.copy(out=dst, in_=src)
-                if c % 2 == 1:
+                if part == 0:
                     nc.sync.dma_start(
-                        out=out[t * P:(t + 1) * P, h * 1024:(h + 1) * 1024],
-                        in_=out_sb[(h, t)][:].rearrange("m r q -> m (r q)"),
+                        out=out[t * P:(t + 1) * P, h0 * 512:(h0 + count) * 512],
+                        in_=res[:, rows, :].rearrange("m r q -> m (r q)"),
                     )

@@ -18,10 +18,9 @@ NG = 4
 NQ = 16
 CHUNK = 8
 
-V_UNITS = [(q, b) for q in (0, 1) for b in range(2)] + [(6, 0)] + [(q, b) for q in range(8, 16) for b in range(2)]
-G_UNITS = [(q, b) for q in (2, 3, 4, 5) for b in range(2)] + [(6, 1)]
-T_Q = 7
-LOADS = [2, 1, 6, 8, 3, 9, 7, 10, 4, 11, "x", 12, 5, 13, 14, 15]
+V_UNITS = [(q, b) for q in (0, 1, 7, 8, 9, 10, 11, 12, 13, 14, 15) for b in range(2)]
+G_UNITS = [(q, b) for q in (2, 3, 4, 5, 6) for b in range(2)]
+LOADS = [2, 1, 7, 8, 3, 9, 10, 4, 11, 12, 5, "x", 13, 14, 6, 15]
 
 
 def tile_lokrlayer_kernel(tc, x, original_weight, lokr_A, lokr_B, scalar, out):
@@ -118,47 +117,30 @@ def tile_lokrlayer_kernel(tc, x, original_weight, lokr_A, lokr_B, scalar, out):
             for g2 in range(2):
                 for u in range(2):
                     w0 = u * 256 + g2 * P
-                    nc.tensor.transpose(
-                        out=bank[:, g2 * 256 + u:(g2 + 1) * 256:2], in_=words[:, w0:w0 + P], identity=ident[:]
-                    )
-            nc.scalar.copy(
-                out=grouped_words[:, 8 * b:8 * (b + 1), q, :],
-                in_=bank[:].rearrange("p (a j) -> p a j", a=8),
-            )
+                    c0 = (g2 * 2 + u) * P
+                    nc.tensor.transpose(out=bank[:, c0:c0 + P], in_=words[:, w0:w0 + P], identity=ident[:])
+            for g2 in range(2):
+                a0 = 4 * (2 * b + g2)
+                nc.scalar.copy(
+                    out=grouped_words[:, a0:a0 + 4, q, :].rearrange("p h (r u) -> p h r u", u=2),
+                    in_=bank[:, g2 * 256:(g2 + 1) * 256].rearrange("p (u h r) -> p h r u", u=2, h=4),
+                )
 
         def transpose_a(b):
             pa = sps.tile([P, 512], F32, name="pa%d" % b, tag="s")
-            transpose_words(pa, a_sb[:].bitcast(F32), b)
-            dst = at[:].bitcast(F32)[:, b * 512:(b + 1) * 512]
+            for g2 in range(2):
+                for u in range(2):
+                    w0 = 256 * (2 * b + g2)
+                    c0 = (g2 * 2 + u) * P
+                    nc.tensor.transpose(
+                        out=pa[:, c0:c0 + P], in_=a_sb[:].bitcast(F32)[:, w0 + u:w0 + 256:2], identity=ident[:]
+                    )
+            dst = at[:].bitcast(F32)[:, b * 512:(b + 1) * 512].rearrange("p (g r u) -> p g r u", g=2, u=2)
+            src = pa[:].rearrange("p (g u r) -> p g r u", g=2, u=2)
             if b == 0:
-                nc.vector.tensor_copy(out=dst, in_=pa[:])
+                nc.vector.tensor_copy(out=dst, in_=src)
             else:
-                nc.scalar.copy(out=dst, in_=pa[:])
-
-        ident_bf = const.tile([P, P], BF16, name="ident_bf")
-        hi = const.tile([P, P], BF16, name="hi")
-        lo = const.tile([P, P], BF16, name="lo")
-        g_hi = const.tile([P, 1], BF16, name="g_hi")
-        g_lo = const.tile([P, 1], F32, name="g_lo")
-
-        def make_diagonals():
-            nc.gpsimd.tensor_copy(out=ident_bf[:], in_=ident[:])
-            nc.vector.tensor_copy(out=g_hi[:], in_=gain[:, T_Q:T_Q + 1])
-            nc.vector.tensor_tensor(out=g_lo[:], in0=gain[:, T_Q:T_Q + 1], in1=g_hi[:], op=ALU.subtract)
-            nc.vector.tensor_scalar(out=hi[:], in0=ident[:], scalar1=gain[:, T_Q:T_Q + 1], scalar2=None, op0=ALU.mult)
-            nc.vector.tensor_scalar(out=lo[:], in0=ident[:], scalar1=g_lo[:, 0:1], scalar2=None, op0=ALU.mult)
-
-        def tensor_pass(g):
-            bank = sps.tile([P, 4, P], F32, name="pt%d" % g, tag="s")
-            for t in range(4):
-                cols = slice(512 * g + t, 512 * (g + 1), 4)
-                nc.tensor.matmul(out=bank[:, t, :], lhsT=w_sb[T_Q][:, cols], rhs=ident_bf[:], start=True, stop=False)
-                nc.tensor.matmul(out=bank[:, t, :], lhsT=a_sb[:, cols], rhs=hi[:], start=False, stop=False)
-                nc.tensor.matmul(out=bank[:, t, :], lhsT=a_sb[:, cols], rhs=lo[:], start=False, stop=True)
-            nc.scalar.copy(
-                out=grouped[0][:, g, :, T_Q, :].rearrange("p h (r t) -> p h r t", t=4),
-                in_=bank[:].rearrange("p t (h r) -> p h r t", h=4),
-            )
+                nc.scalar.copy(out=dst, in_=src)
 
         xg = const.tile([P, 4096], BF16, name="xg", align_bytes=64)
         x_codes = const.tile([P, 1024], U32, name="x_codes", align_bytes=64)
@@ -169,17 +151,19 @@ def tile_lokrlayer_kernel(tc, x, original_weight, lokr_A, lokr_B, scalar, out):
             for t in range(2):
                 for u in range(2):
                     nc.tensor.transpose(
-                        out=px[:, t * 256 + u:(t + 1) * 256:2],
+                        out=px[:, (u * 2 + t) * P:(u * 2 + t + 1) * P],
                         in_=x_sb[:, t, :].bitcast(F32)[:, 256 * g + u:256 * (g + 1):2],
                         identity=ident[:],
                     )
-            nc.scalar.copy(out=xg[:].bitcast(F32)[:, g * 512:(g + 1) * 512], in_=px[:])
+            nc.scalar.copy(
+                out=xg[:].bitcast(F32)[:, g * 512:(g + 1) * 512].rearrange("p (c u) -> p c u", u=2),
+                in_=px[:].rearrange("p (u c) -> p c u", u=2),
+            )
 
         sums = {}
         extras = {}
         for g in range(NG):
-            extras[11 + g] = (tensor_pass, g)
-            extras[16 + g] = (x_pass, g)
+            extras[15 + 2 * g] = (x_pass, g)
         for i in range(len(V_UNITS)):
             q, b = V_UNITS[i]
             if i < 2:
@@ -188,8 +172,6 @@ def tile_lokrlayer_kernel(tc, x, original_weight, lokr_A, lokr_B, scalar, out):
                 make_gain()
             if i % 2 == 0 and i // 2 < len(G_UNITS):
                 sums[i // 2] = delta_add(i // 2)
-            if i == 2:
-                make_diagonals()
             bank = vps.tile([P, 512], F32, name="pv%d" % i, tag="v")
             transpose_words(bank, w_sb[q][:].bitcast(F32), b)
             nc.vector.scalar_tensor_tensor(
@@ -205,6 +187,7 @@ def tile_lokrlayer_kernel(tc, x, original_weight, lokr_A, lokr_B, scalar, out):
             if i in extras:
                 extras[i][0](extras[i][1])
         flush(8, sums[8])
+        flush(9, sums[9])
 
         out_sb = []
         for n in range(4):

@@ -68,14 +68,14 @@ def tile_lokrlayer_kernel(tc, x, original_weight, lokr_A, lokr_B, scalar, out):
             )
 
         def transpose_words(bank, words, b):
-            for g2 in range(2):
-                for u in range(2):
+            for u in range(2):
+                for g2 in range(2):
                     w0 = 256 * (2 * b + g2)
-                    nc.tensor.transpose(
-                        out=bank[:, g2 * 256 + u:(g2 + 1) * 256:2],
-                        in_=words[:, w0 + u:w0 + 256:2],
-                        identity=ident[:],
-                    )
+                    c0 = (u * 2 + g2) * P
+                    nc.tensor.transpose(out=bank[:, c0:c0 + P], in_=words[:, w0 + u:w0 + 256:2], identity=ident[:])
+
+        def by_u(halves):
+            return halves.rearrange("p (u a m) -> p a m u", u=2, a=8)
 
         grouped = [
             const.tile([P, NG, 4, CHUNK, 128], BF16, name="grouped0", align_bytes=64),
@@ -94,17 +94,17 @@ def tile_lokrlayer_kernel(tc, x, original_weight, lokr_A, lokr_B, scalar, out):
         def delta_add(j):
             q, b = G_UNITS[j]
             cols = slice(b * 1024, (b + 1) * 1024)
-            delta = spool.tile([P, 2, 256, 2], F32, name="delta%d" % j, tag="delta", bufs=3)
+            delta = spool.tile([P, 2, 512], F32, name="delta%d" % j, tag="delta", bufs=3)
             nc.scalar.activation(
                 out=delta[:],
-                in_=a_sb[:, cols].rearrange("p (w u e) -> p u w e", u=2, e=2),
+                in_=a_sb[:, cols].rearrange("p (j e) -> p e j", e=2),
                 func=ACT.Copy,
                 scale=gain[:, q:q + 1],
             )
-            wn = spool.tile([P, 2, 256, 2], BF16, name="wn%d" % j, tag="wn", bufs=4)
+            wn = spool.tile([P, 2, 512], BF16, name="wn%d" % j, tag="wn", bufs=4)
             nc.gpsimd.tensor_tensor(
                 out=wn[:],
-                in0=w_sb[q][:, cols].rearrange("p (w u e) -> p u w e", u=2, e=2),
+                in0=w_sb[q][:, cols].rearrange("p (j e) -> p e j", e=2),
                 in1=delta[:],
                 op=ALU.add,
             )
@@ -113,34 +113,22 @@ def tile_lokrlayer_kernel(tc, x, original_weight, lokr_A, lokr_B, scalar, out):
         def flush(j, wn):
             q, b = G_UNITS[j]
             bank = sps.tile([P, 512], F32, name="ps%d" % j, tag="s")
-            words = wn[:].rearrange("p u w e -> p (u w e)").bitcast(F32)
-            for g2 in range(2):
-                for u in range(2):
-                    w0 = u * 256 + g2 * P
-                    c0 = (g2 * 2 + u) * P
-                    nc.tensor.transpose(out=bank[:, c0:c0 + P], in_=words[:, w0:w0 + P], identity=ident[:])
-            for g2 in range(2):
-                a0 = 4 * (2 * b + g2)
-                nc.scalar.copy(
-                    out=grouped_words[:, a0:a0 + 4, q, :].rearrange("p h (r u) -> p h r u", u=2),
-                    in_=bank[:, g2 * 256:(g2 + 1) * 256].rearrange("p (u h r) -> p h r u", u=2, h=4),
-                )
+            words = wn[:].rearrange("p e j -> p (e j)").bitcast(F32)
+            for c0 in range(0, 512, P):
+                nc.tensor.transpose(out=bank[:, c0:c0 + P], in_=words[:, c0:c0 + P], identity=ident[:])
+            nc.scalar.copy(
+                out=grouped_words[:, 8 * b:8 * (b + 1), q, :].rearrange("p a (r e) -> p a r e", e=2),
+                in_=bank[:].rearrange("p (e a r) -> p a r e", e=2, a=8),
+            )
 
         def transpose_a(b):
             pa = sps.tile([P, 512], F32, name="pa%d" % b, tag="s")
-            for g2 in range(2):
-                for u in range(2):
-                    w0 = 256 * (2 * b + g2)
-                    c0 = (g2 * 2 + u) * P
-                    nc.tensor.transpose(
-                        out=pa[:, c0:c0 + P], in_=a_sb[:].bitcast(F32)[:, w0 + u:w0 + 256:2], identity=ident[:]
-                    )
-            dst = at[:].bitcast(F32)[:, b * 512:(b + 1) * 512].rearrange("p (g r u) -> p g r u", g=2, u=2)
-            src = pa[:].rearrange("p (g u r) -> p g r u", g=2, u=2)
+            transpose_words(pa, a_sb[:].bitcast(F32), b)
+            dst = at[:].bitcast(F32)[:, b * 512:(b + 1) * 512]
             if b == 0:
-                nc.vector.tensor_copy(out=dst, in_=src)
+                nc.vector.tensor_copy(out=dst, in_=pa[:])
             else:
-                nc.scalar.copy(out=dst, in_=src)
+                nc.scalar.copy(out=dst, in_=pa[:])
 
         xg = const.tile([P, 4096], BF16, name="xg", align_bytes=64)
         x_codes = const.tile([P, 1024], U32, name="x_codes", align_bytes=64)
@@ -156,8 +144,8 @@ def tile_lokrlayer_kernel(tc, x, original_weight, lokr_A, lokr_B, scalar, out):
                         identity=ident[:],
                     )
             nc.scalar.copy(
-                out=xg[:].bitcast(F32)[:, g * 512:(g + 1) * 512].rearrange("p (c u) -> p c u", u=2),
-                in_=px[:].rearrange("p (u c) -> p c u", u=2),
+                out=xg[:, g * 1024:(g + 1) * 1024].rearrange("p (j u) -> p j u", u=2),
+                in_=px[:].bitcast(BF16).rearrange("p (u j) -> p j u", u=2),
             )
 
         sums = {}
@@ -175,10 +163,10 @@ def tile_lokrlayer_kernel(tc, x, original_weight, lokr_A, lokr_B, scalar, out):
             bank = vps.tile([P, 512], F32, name="pv%d" % i, tag="v")
             transpose_words(bank, w_sb[q][:].bitcast(F32), b)
             nc.vector.scalar_tensor_tensor(
-                out=grouped_slice(q, b),
-                in0=at[:, b * 1024:(b + 1) * 1024].rearrange("p (a j) -> p a j", a=8),
+                out=grouped_slice(q, b).rearrange("p a (m u) -> p a m u", u=2),
+                in0=by_u(at[:, b * 1024:(b + 1) * 1024]),
                 scalar=gain[:, q:q + 1],
-                in1=bank[:].bitcast(BF16).rearrange("p (a j) -> p a j", a=8),
+                in1=by_u(bank[:].bitcast(BF16)),
                 op0=ALU.mult,
                 op1=ALU.add,
             )

@@ -18,9 +18,10 @@ NG = 4
 NQ = 16
 CHUNK = 8
 
-V_UNITS = [(q, b) for q in (0, 1, 7, 8, 9, 10, 11, 12, 13, 14, 15) for b in range(2)]
-G_UNITS = [(q, b) for q in (2, 3, 4, 5, 6) for b in range(2)]
-LOADS = [2, 1, 7, 8, 3, 9, 10, 4, 11, 12, 5, "x", 13, 14, 6, 15]
+V_UNITS = [(0, 0), (1, 0), (0, 1), (1, 1)] + [(q, b) for q in range(8, 16) for b in range(2)] + [(5, 1)]
+G_UNITS = [(q, b) for q in (2, 3, 4) for b in range(2)] + [(5, 0)]
+T_UNITS = [(q, b) for q in (6, 7) for b in range(2)]
+LOADS = [8, 9, 3, 6, 10, 11, 4, 12, "x", 13, 7, 14, 5, 15]
 
 
 def tile_lokrlayer_kernel(tc, x, original_weight, lokr_A, lokr_B, scalar, out):
@@ -45,17 +46,20 @@ def tile_lokrlayer_kernel(tc, x, original_weight, lokr_A, lokr_B, scalar, out):
         nc.scalar.copy(out=warm[:], in_=ones[:, 0:1])
         a_sb = const.tile([P, 2048], BF16, name="a_sb")
         w_rows = original_weight.rearrange("(p q) k -> q p k", q=NQ)
-        w_sb = {0: const.tile([P, 2048], BF16, name="w0")}
+        w_sb = {}
+        for q in (0, 2, 1):
+            w_sb[q] = spool.tile([P, 2048], BF16, name="w%d" % q, tag="w", bufs=13)
         for b in range(2):
             cols = slice(b * 1024, (b + 1) * 1024)
             nc.sync.dma_start(out=a_sb[:, cols], in_=lokr_A[:, cols])
-            nc.sync.dma_start(out=w_sb[0][:, cols], in_=w_rows[0][:, cols])
+            for q in (0, 2, 1):
+                nc.sync.dma_start(out=w_sb[q][:, cols], in_=w_rows[q][:, cols])
         x_sb = const.tile([P, 2, 2048], BF16, name="x_sb")
         for q in LOADS:
             if q == "x":
                 nc.sync.dma_start(out=x_sb[:], in_=x.rearrange("(t m) k -> m t k", t=2))
             else:
-                w_sb[q] = const.tile([P, 2048], BF16, name="w%d" % q)
+                w_sb[q] = spool.tile([P, 2048], BF16, name="w%d" % q, tag="w", bufs=13)
                 nc.sync.dma_start(out=w_sb[q][:], in_=w_rows[q])
 
         gain = const.tile([P, NQ], F32, name="gain")
@@ -130,6 +134,41 @@ def tile_lokrlayer_kernel(tc, x, original_weight, lokr_A, lokr_B, scalar, out):
             else:
                 nc.scalar.copy(out=dst, in_=pa[:])
 
+        ident_bf = const.tile([P, P], BF16, name="ident_bf")
+        nc.gpsimd.tensor_copy(out=ident_bf[:], in_=ident[:])
+
+        def make_delta(n):
+            q, b = T_UNITS[n]
+            delta = spool.tile([P, 4, 256], F32, name="tdelta%d" % n, tag="tdelta", bufs=2)
+            nc.gpsimd.tensor_scalar(
+                out=delta[:],
+                in0=a_sb[:, b * 1024:(b + 1) * 1024].rearrange("p (w t) -> p t w", t=4),
+                scalar1=gain[:, q:q + 1],
+                scalar2=0.0,
+                op0=ALU.mult,
+                op1=ALU.add,
+            )
+            return delta
+
+        def tensor_sum(n, g2):
+            q, b = T_UNITS[n]
+            g = 2 * b + g2
+            bank = sps.tile([P, 4, P], F32, name="pt%d_%d" % (n, g2), tag="s")
+            for e in range(2):
+                for u in range(2):
+                    t = 2 * u + e
+                    column = bank[:, 2 * e + u, :]
+                    nc.tensor.matmul(
+                        out=column, lhsT=deltas[n][:, t, g2 * P:(g2 + 1) * P], rhs=ident[:], start=True, stop=False, is_transpose=True
+                    )
+                    nc.tensor.matmul(
+                        out=column, lhsT=w_sb[q][:, 512 * g + t:512 * (g + 1):4], rhs=ident_bf[:], start=False, stop=True
+                    )
+            nc.scalar.copy(
+                out=grouped[0][:, g, :, q, :].rearrange("p h (r t) -> p h r t", t=4),
+                in_=bank[:].rearrange("p t (h r) -> p h r t", h=4),
+            )
+
         xg = const.tile([P, 4096], BF16, name="xg", align_bytes=64)
         x_codes = const.tile([P, 1024], U32, name="x_codes", align_bytes=64)
         x_scales = const.tile([P, 1024], U8, name="x_scales", align_bytes=64)
@@ -149,17 +188,24 @@ def tile_lokrlayer_kernel(tc, x, original_weight, lokr_A, lokr_B, scalar, out):
             )
 
         sums = {}
-        extras = {}
-        for g in range(NG):
-            extras[15 + 2 * g] = (x_pass, g)
+        deltas = {}
         for i in range(len(V_UNITS)):
             q, b = V_UNITS[i]
-            if i < 2:
-                transpose_a(i)
             if i == 0:
+                transpose_a(0)
                 make_gain()
-            if i % 2 == 0 and i // 2 < len(G_UNITS):
-                sums[i // 2] = delta_add(i // 2)
+            if i == 2:
+                transpose_a(1)
+            if i % 5 == 0 and i // 5 < len(T_UNITS):
+                deltas[i // 5] = make_delta(i // 5)
+            if i % 3 == 0:
+                sums[i // 3] = delta_add(i // 3)
+            if i >= 6 and i % 3 == 0:
+                flush(i // 3 - 2, sums[i // 3 - 2])
+            if i >= 9 and i % 5 in (4, 0):
+                tensor_sum((i - 9) // 5, (i - 9) % 5)
+            if i >= 13 and i % 5 in (2, 3) and i < 19:
+                x_pass((13, 17, 18).index(i))
             bank = vps.tile([P, 512], F32, name="pv%d" % i, tag="v")
             transpose_words(bank, w_sb[q][:].bitcast(F32), b)
             nc.vector.scalar_tensor_tensor(
@@ -170,12 +216,11 @@ def tile_lokrlayer_kernel(tc, x, original_weight, lokr_A, lokr_B, scalar, out):
                 op0=ALU.mult,
                 op1=ALU.add,
             )
-            if i >= 6 and i % 2 == 0:
-                flush((i - 6) // 2, sums[(i - 6) // 2])
-            if i in extras:
-                extras[i][0](extras[i][1])
-        flush(8, sums[8])
-        flush(9, sums[9])
+        x_pass(3)
+        flush(5, sums[5])
+        for g2 in range(2):
+            tensor_sum(3, g2)
+        flush(6, sums[6])
 
         out_sb = []
         for n in range(4):

@@ -18,10 +18,11 @@ NG = 4
 NQ = 16
 CHUNK = 8
 
-V_UNITS = [(0, 0), (1, 0), (0, 1), (1, 1)] + [(q, b) for q in range(8, 16) for b in range(2)] + [(5, 1)]
-G_UNITS = [(q, b) for q in (2, 3, 4) for b in range(2)] + [(5, 0)]
-T_UNITS = [(q, b) for q in (6, 7) for b in range(2)]
-LOADS = [8, 9, 3, 6, 10, 11, 4, 12, "x", 13, 7, 14, 5, 15]
+V_UNITS = [(0, 0), (1, 0), (0, 1)] + [(q, b) for q in range(8, 16) for b in range(2)]
+G_UNITS = [(2, 0), (2, 1), (1, 1)] + [(q, b) for q in (3, 4, 5) for b in range(2)]
+PAIR = 6
+HALVES = [("a", 0), (0, 0), (2, 0), (1, 0), ("a", 1), (0, 1), (2, 1), (8, 0), (8, 1), (1, 1)]
+LOADS = [9, 10, 3, 11, 12, 4, 13, "x", 14, 5, 15]
 
 
 def tile_lokrlayer_kernel(tc, x, original_weight, lokr_A, lokr_B, scalar, out):
@@ -47,20 +48,26 @@ def tile_lokrlayer_kernel(tc, x, original_weight, lokr_A, lokr_B, scalar, out):
         a_sb = const.tile([P, 2048], BF16, name="a_sb")
         w_rows = original_weight.rearrange("(p q) k -> q p k", q=NQ)
         w_sb = {}
-        for q in (0, 2, 1):
-            w_sb[q] = spool.tile([P, 2048], BF16, name="w%d" % q, tag="w", bufs=13)
-        for b in range(2):
+        for q, b in HALVES:
             cols = slice(b * 1024, (b + 1) * 1024)
-            nc.sync.dma_start(out=a_sb[:, cols], in_=lokr_A[:, cols])
-            for q in (0, 2, 1):
-                nc.sync.dma_start(out=w_sb[q][:, cols], in_=w_rows[q][:, cols])
+            if q == "a":
+                nc.sync.dma_start(out=a_sb[:, cols], in_=lokr_A[:, cols])
+                continue
+            if b == 0:
+                w_sb[q] = spool.tile([P, 2048], BF16, name="w%d" % q, tag="w", bufs=12)
+            nc.sync.dma_start(out=w_sb[q][:, cols], in_=w_rows[q][:, cols])
         x_sb = const.tile([P, 2, 2048], BF16, name="x_sb")
         for q in LOADS:
             if q == "x":
                 nc.sync.dma_start(out=x_sb[:], in_=x.rearrange("(t m) k -> m t k", t=2))
             else:
-                w_sb[q] = spool.tile([P, 2048], BF16, name="w%d" % q, tag="w", bufs=13)
+                w_sb[q] = spool.tile([P, 2048], BF16, name="w%d" % q, tag="w", bufs=12)
                 nc.sync.dma_start(out=w_sb[q][:], in_=w_rows[q])
+        mixed = const.tile([P, 4, 2048], BF16, name="mixed")
+        for b in range(2):
+            cols = slice(b * 1024, (b + 1) * 1024)
+            for role, rows in enumerate((w_rows[PAIR], w_rows[PAIR + 1], lokr_A, lokr_A)):
+                nc.sync.dma_start(out=mixed[role:P:4, :, cols], in_=rows.rearrange("(h m) k -> m h k", h=4)[:, :, cols])
 
         gain = const.tile([P, NQ], F32, name="gain")
 
@@ -134,39 +141,48 @@ def tile_lokrlayer_kernel(tc, x, original_weight, lokr_A, lokr_B, scalar, out):
             else:
                 nc.scalar.copy(out=dst, in_=pa[:])
 
-        ident_bf = const.tile([P, P], BF16, name="ident_bf")
-        nc.gpsimd.tensor_copy(out=ident_bf[:], in_=ident[:])
+        same_row = const.tile([P, 32], F32, name="same_row")
+        roles = const.tile([P, 4], F32, name="roles")
+        nc.vector.tensor_reduce(out=same_row[:], in_=ident[:].rearrange("p (m r) -> p m r", r=4), op=ALU.add, axis=mybir.AxisListType.X)
+        nc.vector.tensor_reduce(out=roles[:], in_=ident[:].rearrange("p (m r) -> p r m", r=4), op=ALU.add, axis=mybir.AxisListType.X)
+        g_hi = const.tile([P, 2], BF16, name="g_hi")
+        g_lo = const.tile([P, 2], F32, name="g_lo")
+        part = const.tile([P, 2], F32, name="part")
+        weight = const.tile([P, 2], F32, name="weight")
+        mixer = const.tile([P, 64], BF16, name="mixer")
 
-        def make_delta(n):
-            q, b = T_UNITS[n]
-            delta = spool.tile([P, 4, 256], F32, name="tdelta%d" % n, tag="tdelta", bufs=2)
-            nc.gpsimd.tensor_scalar(
-                out=delta[:],
-                in0=a_sb[:, b * 1024:(b + 1) * 1024].rearrange("p (w t) -> p t w", t=4),
-                scalar1=gain[:, q:q + 1],
-                scalar2=0.0,
-                op0=ALU.mult,
-                op1=ALU.add,
+        def make_mixer():
+            pair = gain[:, PAIR:PAIR + 2]
+            nc.vector.tensor_copy(out=g_hi[:], in_=pair)
+            nc.vector.tensor_tensor(out=g_lo[:], in0=pair, in1=g_hi[:], op=ALU.subtract)
+            nc.vector.scalar_tensor_tensor(
+                out=part[:], in0=g_hi[:], scalar=roles[:, 2:3], in1=roles[:, 0:2], op0=ALU.mult, op1=ALU.add
             )
-            return delta
+            nc.vector.scalar_tensor_tensor(
+                out=weight[:], in0=g_lo[:], scalar=roles[:, 3:4], in1=part[:], op0=ALU.mult, op1=ALU.add
+            )
+            for j in range(2):
+                nc.vector.tensor_scalar(
+                    out=mixer[:, j * 32:(j + 1) * 32], in0=same_row[:], scalar1=weight[:, j:j + 1], scalar2=None, op0=ALU.mult
+                )
 
-        def tensor_sum(n, g2):
-            q, b = T_UNITS[n]
-            g = 2 * b + g2
-            bank = sps.tile([P, 4, P], F32, name="pt%d_%d" % (n, g2), tag="s")
+        def pair_pass(g):
+            bank = sps.tile([P, 4, 256], BF16, name="pt%d" % g, tag="s")
             for e in range(2):
                 for u in range(2):
                     t = 2 * u + e
-                    column = bank[:, 2 * e + u, :]
-                    nc.tensor.matmul(
-                        out=column, lhsT=deltas[n][:, t, g2 * P:(g2 + 1) * P], rhs=ident[:], start=True, stop=False, is_transpose=True
-                    )
-                    nc.tensor.matmul(
-                        out=column, lhsT=w_sb[q][:, 512 * g + t:512 * (g + 1):4], rhs=ident_bf[:], start=False, stop=True
-                    )
+                    for h in range(4):
+                        nc.tensor.matmul(
+                            out=bank[:, 2 * e + u, h * 64:(h + 1) * 64],
+                            lhsT=mixed[:, h, 512 * g + t:512 * (g + 1):4],
+                            rhs=mixer[:],
+                            start=True,
+                            stop=True,
+                        )
+            rows = grouped[0][:].rearrange("p g h q j -> p g h (q j)")[:, g, :, PAIR * 128:(PAIR + 2) * 128]
             nc.scalar.copy(
-                out=grouped[0][:, g, :, q, :].rearrange("p h (r t) -> p h r t", t=4),
-                in_=bank[:].rearrange("p t (h r) -> p h r t", h=4),
+                out=rows.rearrange("p h (m t) -> p h m t", t=4),
+                in_=bank[:].rearrange("p t (h m) -> p h m t", h=4),
             )
 
         xg = const.tile([P, 4096], BF16, name="xg", align_bytes=64)
@@ -188,24 +204,21 @@ def tile_lokrlayer_kernel(tc, x, original_weight, lokr_A, lokr_B, scalar, out):
             )
 
         sums = {}
-        deltas = {}
         for i in range(len(V_UNITS)):
             q, b = V_UNITS[i]
             if i == 0:
-                transpose_a(0)
                 make_gain()
+                make_mixer()
+                transpose_a(0)
+            for j in range(len(G_UNITS)):
+                if i == 2 * j:
+                    sums[j] = delta_add(j)
+                if i == 9 * j // 4 + 6:
+                    flush(j, sums[j])
             if i == 2:
                 transpose_a(1)
-            if i % 5 == 0 and i // 5 < len(T_UNITS):
-                deltas[i // 5] = make_delta(i // 5)
-            if i % 3 == 0:
-                sums[i // 3] = delta_add(i // 3)
-            if i >= 6 and i % 3 == 0:
-                flush(i // 3 - 2, sums[i // 3 - 2])
-            if i >= 9 and i % 5 in (4, 0):
-                tensor_sum((i - 9) // 5, (i - 9) % 5)
-            if i >= 13 and i % 5 in (2, 3) and i < 19:
-                x_pass((13, 17, 18).index(i))
+            if i >= 15:
+                x_pass(i - 15)
             bank = vps.tile([P, 512], F32, name="pv%d" % i, tag="v")
             transpose_words(bank, w_sb[q][:].bitcast(F32), b)
             nc.vector.scalar_tensor_tensor(
@@ -216,11 +229,13 @@ def tile_lokrlayer_kernel(tc, x, original_weight, lokr_A, lokr_B, scalar, out):
                 op0=ALU.mult,
                 op1=ALU.add,
             )
-        x_pass(3)
-        flush(5, sums[5])
-        for g2 in range(2):
-            tensor_sum(3, g2)
         flush(6, sums[6])
+        flush(7, sums[7])
+        pair_pass(0)
+        pair_pass(1)
+        flush(8, sums[8])
+        pair_pass(2)
+        pair_pass(3)
 
         out_sb = []
         for n in range(4):

@@ -18,11 +18,11 @@ NG = 4
 NQ = 16
 CHUNK = 8
 
-V_UNITS = [(0, 0), (1, 0), (0, 1)] + [(q, b) for q in range(8, 16) for b in range(2)]
+V_UNITS = [(0, 0), (1, 0), (0, 1)] + [(q, b) for q in range(8, 16) for b in range(2)] + [(6, 1), (7, 1)]
 G_UNITS = [(2, 0), (2, 1), (1, 1)] + [(q, b) for q in (3, 4, 5) for b in range(2)]
 PAIR = 6
 HALVES = [("a", 0), (0, 0), (2, 0), (1, 0), ("a", 1), (0, 1), (2, 1), (8, 0), (8, 1), (1, 1)]
-LOADS = [9, 10, 3, 11, 12, 4, 13, "x", 14, 5, 15]
+LOADS = [9, 3, 10, 11, 12, 4, 13, "x", 14, 5, 15, "m", (6, 1), (7, 1)]
 
 
 def tile_lokrlayer_kernel(tc, x, original_weight, lokr_A, lokr_B, scalar, out):
@@ -57,17 +57,19 @@ def tile_lokrlayer_kernel(tc, x, original_weight, lokr_A, lokr_B, scalar, out):
                 w_sb[q] = spool.tile([P, 2048], BF16, name="w%d" % q, tag="w", bufs=12)
             nc.sync.dma_start(out=w_sb[q][:, cols], in_=w_rows[q][:, cols])
         x_sb = const.tile([P, 2, 2048], BF16, name="x_sb")
+        mixed = const.tile([P, 4, 1024], BF16, name="mixed")
         for q in LOADS:
             if q == "x":
                 nc.sync.dma_start(out=x_sb[:], in_=x.rearrange("(t m) k -> m t k", t=2))
+            elif q == "m":
+                for role, rows in enumerate((w_rows[PAIR], w_rows[PAIR + 1], lokr_A, lokr_A)):
+                    nc.sync.dma_start(out=mixed[role:P:4, :, :], in_=rows.rearrange("(h m) k -> m h k", h=4)[:, :, 0:1024])
+            elif q in ((6, 1), (7, 1)):
+                w_sb[q[0]] = spool.tile([P, 2048], BF16, name="w%d" % q[0], tag="w", bufs=12)
+                nc.sync.dma_start(out=w_sb[q[0]][:, 1024:2048], in_=w_rows[q[0]][:, 1024:2048])
             else:
                 w_sb[q] = spool.tile([P, 2048], BF16, name="w%d" % q, tag="w", bufs=12)
                 nc.sync.dma_start(out=w_sb[q][:], in_=w_rows[q])
-        mixed = const.tile([P, 4, 2048], BF16, name="mixed")
-        for b in range(2):
-            cols = slice(b * 1024, (b + 1) * 1024)
-            for role, rows in enumerate((w_rows[PAIR], w_rows[PAIR + 1], lokr_A, lokr_A)):
-                nc.sync.dma_start(out=mixed[role:P:4, :, cols], in_=rows.rearrange("(h m) k -> m h k", h=4)[:, :, cols])
 
         gain = const.tile([P, NQ], F32, name="gain")
 
@@ -166,19 +168,24 @@ def tile_lokrlayer_kernel(tc, x, original_weight, lokr_A, lokr_B, scalar, out):
                     out=mixer[:, j * 32:(j + 1) * 32], in0=same_row[:], scalar1=weight[:, j:j + 1], scalar2=None, op0=ALU.mult
                 )
 
-        def pair_pass(g):
-            bank = sps.tile([P, 4, 256], BF16, name="pt%d" % g, tag="s")
-            for e in range(2):
-                for u in range(2):
-                    t = 2 * u + e
-                    for h in range(4):
-                        nc.tensor.matmul(
-                            out=bank[:, 2 * e + u, h * 64:(h + 1) * 64],
-                            lhsT=mixed[:, h, 512 * g + t:512 * (g + 1):4],
-                            rhs=mixer[:],
-                            start=True,
-                            stop=True,
-                        )
+        pair_banks = {}
+
+        def pair_half(g, e):
+            if e == 0:
+                pair_banks[g] = sps.tile([P, 4, 256], BF16, name="pt%d" % g, tag="s")
+            bank = pair_banks[g]
+            for u in range(2):
+                t = 2 * u + e
+                for h in range(4):
+                    nc.tensor.matmul(
+                        out=bank[:, 2 * e + u, h * 64:(h + 1) * 64],
+                        lhsT=mixed[:, h, 512 * g + t:512 * (g + 1):4],
+                        rhs=mixer[:],
+                        start=True,
+                        stop=True,
+                    )
+            if e == 0:
+                return
             rows = grouped[0][:].rearrange("p g h q j -> p g h (q j)")[:, g, :, PAIR * 128:(PAIR + 2) * 128]
             nc.scalar.copy(
                 out=rows.rearrange("p h (m t) -> p h m t", t=4),
@@ -217,8 +224,10 @@ def tile_lokrlayer_kernel(tc, x, original_weight, lokr_A, lokr_B, scalar, out):
                     flush(j, sums[j])
             if i == 2:
                 transpose_a(1)
-            if i >= 15:
+            if 15 <= i < 19:
                 x_pass(i - 15)
+            if i == 20:
+                pair_half(0, 0)
             bank = vps.tile([P, 512], F32, name="pv%d" % i, tag="v")
             transpose_words(bank, w_sb[q][:].bitcast(F32), b)
             nc.vector.scalar_tensor_tensor(
@@ -229,13 +238,11 @@ def tile_lokrlayer_kernel(tc, x, original_weight, lokr_A, lokr_B, scalar, out):
                 op0=ALU.mult,
                 op1=ALU.add,
             )
-        flush(6, sums[6])
         flush(7, sums[7])
-        pair_pass(0)
-        pair_pass(1)
+        pair_half(0, 1)
+        pair_half(1, 0)
+        pair_half(1, 1)
         flush(8, sums[8])
-        pair_pass(2)
-        pair_pass(3)
 
         out_sb = []
         for n in range(4):

@@ -18,11 +18,11 @@ NG = 4
 NQ = 16
 CHUNK = 8
 
-V_UNITS = [(0, 0), (1, 0), (0, 1)] + [(q, b) for q in range(8, 16) for b in range(2)] + [(6, 1), (7, 1)]
-G_UNITS = [(2, 0), (2, 1), (1, 1)] + [(q, b) for q in (3, 4, 5) for b in range(2)]
+V_UNITS = [(0, 0), (1, 0), (0, 1)] + [(q, b) for q in range(8, 16) for b in range(2)] + [(7, 1)]
+G_UNITS = [(2, 0), (2, 1), (1, 1)] + [(q, b) for q in (3, 4, 5) for b in range(2)] + [(6, 1)]
 PAIR = 6
 HALVES = [("a", 0), (0, 0), (2, 0), (1, 0), ("a", 1), (0, 1), (2, 1), (8, 0), (8, 1), (1, 1)]
-LOADS = [9, 3, 10, 11, 12, 4, 13, "x", 14, 5, 15, "m", (6, 1), (7, 1)]
+LOADS = [9, 3, 10, 11, 12, 4, 13, "x", 14, 5, 15, (7, 1), (6, 1), "m"]
 
 
 def tile_lokrlayer_kernel(tc, x, original_weight, lokr_A, lokr_B, scalar, out):
@@ -226,8 +226,6 @@ def tile_lokrlayer_kernel(tc, x, original_weight, lokr_A, lokr_B, scalar, out):
                 transpose_a(1)
             if 15 <= i < 19:
                 x_pass(i - 15)
-            if i == 20:
-                pair_half(0, 0)
             bank = vps.tile([P, 512], F32, name="pv%d" % i, tag="v")
             transpose_words(bank, w_sb[q][:].bitcast(F32), b)
             nc.vector.scalar_tensor_tensor(
@@ -239,10 +237,12 @@ def tile_lokrlayer_kernel(tc, x, original_weight, lokr_A, lokr_B, scalar, out):
                 op1=ALU.add,
             )
         flush(7, sums[7])
+        flush(8, sums[8])
+        pair_half(0, 0)
         pair_half(0, 1)
+        flush(9, sums[9])
         pair_half(1, 0)
         pair_half(1, 1)
-        flush(8, sums[8])
 
         out_sb = []
         for n in range(4):

from contextlib import ExitStack

import concourse.mybir as mybir
from concourse.masks import make_identity

FP8X4 = mybir.dt.float8_e4m3fn_x4
BF16 = mybir.dt.bfloat16
F32 = mybir.dt.float32
U32 = mybir.dt.uint32
U8 = mybir.dt.uint8
ALU = mybir.AluOpType
ACT = mybir.ActivationFunctionType

FLOPS = 2 * 256 * 2048 * 2048

P = 128
NG = 4
NQ = 16
CHUNK = 8

V_UNITS = [(0, 0), (1, 0), (0, 1)] + [(q, b) for q in range(8, 16) for b in range(2)] + [(7, 1)]
G_UNITS = [(2, 0), (2, 1), (1, 1)] + [(q, b) for q in (3, 4, 5) for b in range(2)] + [(6, 1)]
PAIR = 6
HALVES = [("a", 0), (0, 0), (2, 0), (1, 0), ("a", 1), (0, 1), (2, 1), (8, 0), (8, 1), (1, 1)]
LOADS = [9, 3, 10, 11, 12, 4, 13, "x", 14, 5, 15, (7, 1), (6, 1), "m"]


def tile_lokrlayer_kernel(tc, x, original_weight, lokr_A, lokr_B, scalar, out):
    nc = tc.nc
    with ExitStack() as ctx:
        const = ctx.enter_context(tc.tile_pool(name="const", bufs=1))
        spool = ctx.enter_context(tc.tile_pool(name="spool", bufs=1))
        vps = ctx.enter_context(tc.psum_pool(name="vps", bufs=4))
        sps = ctx.enter_context(tc.psum_pool(name="sps", bufs=4))
        ctx.enter_context(tc.manual_schedule())

        ident = const.tile([P, P], F32, name="ident")
        make_identity(nc, ident[:])

        small = const.tile([P, 2 * NQ], BF16, name="small")
        nc.vector.memset(small[:], 0.0)
        ones = const.tile([P, P], BF16, name="ones")
        nc.vector.memset(ones[:], 1.0)
        nc.sync.dma_start(out=small[0:1, 0:NQ], in_=lokr_B.rearrange("q o -> o q"))
        nc.sync.dma_start(out=small[0:1, NQ:NQ + 1], in_=scalar.unsqueeze(0))
        warm = const.tile([P, 1], F32, name="warm")
        nc.scalar.copy(out=warm[:], in_=ones[:, 0:1])
        a_sb = const.tile([P, 2048], BF16, name="a_sb")
        w_rows = original_weight.rearrange("(p q) k -> q p k", q=NQ)
        w_sb = {}
        for q, b in HALVES:
            cols = slice(b * 1024, (b + 1) * 1024)
            if q == "a":
                nc.sync.dma_start(out=a_sb[:, cols], in_=lokr_A[:, cols])
                continue
            if b == 0:
                w_sb[q] = spool.tile([P, 2048], BF16, name="w%d" % q, tag="w", bufs=12)
            nc.sync.dma_start(out=w_sb[q][:, cols], in_=w_rows[q][:, cols])
        x_sb = const.tile([P, 2, 2048], BF16, name="x_sb")
        mixed = const.tile([P, 4, 1024], BF16, name="mixed")
        for q in LOADS:
            if q == "x":
                nc.sync.dma_start(out=x_sb[:], in_=x.rearrange("(t m) k -> m t k", t=2))
            elif q == "m":
                for role, rows in enumerate((w_rows[PAIR], w_rows[PAIR + 1], lokr_A, lokr_A)):
                    nc.sync.dma_start(out=mixed[role:P:4, :, :], in_=rows.rearrange("(h m) k -> m h k", h=4)[:, :, 0:1024])
            elif q in ((6, 1), (7, 1)):
                w_sb[q[0]] = spool.tile([P, 2048], BF16, name="w%d" % q[0], tag="w", bufs=12)
                nc.sync.dma_start(out=w_sb[q[0]][:, 1024:2048], in_=w_rows[q[0]][:, 1024:2048])
            else:
                w_sb[q] = spool.tile([P, 2048], BF16, name="w%d" % q, tag="w", bufs=12)
                nc.sync.dma_start(out=w_sb[q][:], in_=w_rows[q])

        gain = const.tile([P, NQ], F32, name="gain")

        def make_gain():
            spread = vps.tile([P, 2 * NQ], F32, name="spread", tag="v")
            nc.tensor.matmul(out=spread[:], lhsT=ones[:], rhs=small[:], start=True, stop=True)
            nc.vector.tensor_scalar(
                out=gain[:], in0=spread[:, 0:NQ], scalar1=spread[:, NQ:NQ + 1], scalar2=2.0, op0=ALU.mult, op1=ALU.mult
            )

        def transpose_words(bank, words, b):
            for u in range(2):
                for g2 in range(2):
                    w0 = 256 * (2 * b + g2)
                    c0 = (u * 2 + g2) * P
                    nc.tensor.transpose(out=bank[:, c0:c0 + P], in_=words[:, w0 + u:w0 + 256:2], identity=ident[:])

        def by_u(halves):
            return halves.rearrange("p (u a m) -> p a m u", u=2, a=8)

        grouped = [
            const.tile([P, NG, 4, CHUNK, 128], BF16, name="grouped0", align_bytes=64),
            const.tile([P, NG, 4, CHUNK, 128], BF16, name="grouped1", align_bytes=64),
        ]
        grouped_words = grouped[0][:].rearrange("p g h q j -> p (g h q j)").bitcast(F32).rearrange(
            "p (a q j) -> p a q j", a=4 * NG, q=CHUNK
        )

        def grouped_slice(q, b):
            tile = grouped[q // CHUNK]
            return tile[:].rearrange("p g h q j -> p (g h) q j")[:, 8 * b:8 * (b + 1), q % CHUNK, :]

        at = const.tile([P, 2048], BF16, name="at")

        def delta_add(j):
            q, b = G_UNITS[j]
            cols = slice(b * 1024, (b + 1) * 1024)
            delta = spool.tile([P, 2, 512], F32, name="delta%d" % j, tag="delta", bufs=3)
            nc.scalar.activation(
                out=delta[:],
                in_=a_sb[:, cols].rearrange("p (j e) -> p e j", e=2),
                func=ACT.Copy,
                scale=gain[:, q:q + 1],
            )
            wn = spool.tile([P, 2, 512], BF16, name="wn%d" % j, tag="wn", bufs=4)
            nc.gpsimd.tensor_tensor(
                out=wn[:],
                in0=w_sb[q][:, cols].rearrange("p (j e) -> p e j", e=2),
                in1=delta[:],
                op=ALU.add,
            )
            return wn

        def flush(j, wn):
            q, b = G_UNITS[j]
            bank = sps.tile([P, 512], F32, name="ps%d" % j, tag="s")
            words = wn[:].rearrange("p e j -> p (e j)").bitcast(F32)
            for c0 in range(0, 512, P):
                nc.tensor.transpose(out=bank[:, c0:c0 + P], in_=words[:, c0:c0 + P], identity=ident[:])
            nc.scalar.copy(
                out=grouped_words[:, 8 * b:8 * (b + 1), q, :].rearrange("p a (r e) -> p a r e", e=2),
                in_=bank[:].rearrange("p (e a r) -> p a r e", e=2, a=8),
            )

        def transpose_a(b):
            pa = sps.tile([P, 512], F32, name="pa%d" % b, tag="s")
            transpose_words(pa, a_sb[:].bitcast(F32), b)
            dst = at[:].bitcast(F32)[:, b * 512:(b + 1) * 512]
            if b == 0:
                nc.vector.tensor_copy(out=dst, in_=pa[:])
            else:
                nc.scalar.copy(out=dst, in_=pa[:])

        same_row = const.tile([P, 32], F32, name="same_row")
        roles = const.tile([P, 4], F32, name="roles")
        nc.vector.tensor_reduce(out=same_row[:], in_=ident[:].rearrange("p (m r) -> p m r", r=4), op=ALU.add, axis=mybir.AxisListType.X)
        nc.vector.tensor_reduce(out=roles[:], in_=ident[:].rearrange("p (m r) -> p r m", r=4), op=ALU.add, axis=mybir.AxisListType.X)
        g_hi = const.tile([P, 2], BF16, name="g_hi")
        g_lo = const.tile([P, 2], F32, name="g_lo")
        part = const.tile([P, 2], F32, name="part")
        weight = const.tile([P, 2], F32, name="weight")
        mixer = const.tile([P, 64], BF16, name="mixer")

        def make_mixer():
            pair = gain[:, PAIR:PAIR + 2]
            nc.vector.tensor_copy(out=g_hi[:], in_=pair)
            nc.vector.tensor_tensor(out=g_lo[:], in0=pair, in1=g_hi[:], op=ALU.subtract)
            nc.vector.scalar_tensor_tensor(
                out=part[:], in0=g_hi[:], scalar=roles[:, 2:3], in1=roles[:, 0:2], op0=ALU.mult, op1=ALU.add
            )
            nc.vector.scalar_tensor_tensor(
                out=weight[:], in0=g_lo[:], scalar=roles[:, 3:4], in1=part[:], op0=ALU.mult, op1=ALU.add
            )
            for j in range(2):
                nc.vector.tensor_scalar(
                    out=mixer[:, j * 32:(j + 1) * 32], in0=same_row[:], scalar1=weight[:, j:j + 1], scalar2=None, op0=ALU.mult
                )

        pair_banks = {}

        def pair_half(g, e):
            if e == 0:
                pair_banks[g] = sps.tile([P, 4, 256], BF16, name="pt%d" % g, tag="s")
            bank = pair_banks[g]
            for u in range(2):
                t = 2 * u + e
                for h in range(4):
                    nc.tensor.matmul(
                        out=bank[:, 2 * e + u, h * 64:(h + 1) * 64],
                        lhsT=mixed[:, h, 512 * g + t:512 * (g + 1):4],
                        rhs=mixer[:],
                        start=True,
                        stop=True,
                    )
            if e == 0:
                return
            rows = grouped[0][:].rearrange("p g h q j -> p g h (q j)")[:, g, :, PAIR * 128:(PAIR + 2) * 128]
            nc.scalar.copy(
                out=rows.rearrange("p h (m t) -> p h m t", t=4),
                in_=bank[:].rearrange("p t (h m) -> p h m t", h=4),
            )

        xg = const.tile([P, 4096], BF16, name="xg", align_bytes=64)
        x_codes = const.tile([P, 1024], U32, name="x_codes", align_bytes=64)
        x_scales = const.tile([P, 1024], U8, name="x_scales", align_bytes=64)

        def x_pass(g):
            px = sps.tile([P, 512], F32, name="px%d" % g, tag="s")
            for t in range(2):
                for u in range(2):
                    nc.tensor.transpose(
                        out=px[:, (u * 2 + t) * P:(u * 2 + t + 1) * P],
                        in_=x_sb[:, t, :].bitcast(F32)[:, 256 * g + u:256 * (g + 1):2],
                        identity=ident[:],
                    )
            nc.scalar.copy(
                out=xg[:, g * 1024:(g + 1) * 1024].rearrange("p (j u) -> p j u", u=2),
                in_=px[:].bitcast(BF16).rearrange("p (u j) -> p j u", u=2),
            )

        sums = {}
        for i in range(len(V_UNITS)):
            q, b = V_UNITS[i]
            if i == 0:
                make_gain()
                make_mixer()
                transpose_a(0)
            for j in range(len(G_UNITS)):
                if i == 2 * j:
                    sums[j] = delta_add(j)
                if i == 9 * j // 4 + 6:
                    flush(j, sums[j])
            if i == 2:
                transpose_a(1)
            if 15 <= i < 19:
                x_pass(i - 15)
            bank = vps.tile([P, 512], F32, name="pv%d" % i, tag="v")
            transpose_words(bank, w_sb[q][:].bitcast(F32), b)
            nc.vector.scalar_tensor_tensor(
                out=grouped_slice(q, b).rearrange("p a (m u) -> p a m u", u=2),
                in0=by_u(at[:, b * 1024:(b + 1) * 1024]),
                scalar=gain[:, q:q + 1],
                in1=by_u(bank[:].bitcast(BF16)),
                op0=ALU.mult,
                op1=ALU.add,
            )
        flush(7, sums[7])
        flush(8, sums[8])
        pair_half(0, 0)
        pair_half(0, 1)
        flush(9, sums[9])
        pair_half(1, 0)
        pair_half(1, 1)

        out_sb = []
        for n in range(4):
            out_tile = const.tile([P, 64, NQ], F32, name="out_sb%d" % n)
            out_sb.append(out_tile)
        chunks = [(1, 0, 2), (0, 0, 2), (1, 2, 2), (0, 2, 1), (0, 3, 1)]
        for c, (part, h0, count) in enumerate(chunks):
            width = count * CHUNK * 32
            codes = const.tile([P, NG, width], U32, name="codes%d" % c, align_bytes=64)
            scales = const.tile([P, NG, width], U8, name="scales%d" % c, align_bytes=64)
            accs = [
                vps.tile([P, width], F32, name="acc%d_0" % c, tag="v"),
                sps.tile([P, width], F32, name="acc%d_1" % c, tag="s"),
            ]
            for g in range(NG):
                if c == 0:
                    nc.vector.quantize_mx(
                        out=x_codes[:, g * 256:(g + 1) * 256].bitcast(FP8X4),
                        scales=x_scales[:, g * 256:(g + 1) * 256],
                        in_=xg[:, g * 1024:(g + 1) * 1024],
                    )
                nc.vector.quantize_mx(
                    out=codes[:, g, :].bitcast(FP8X4),
                    scales=scales[:, g, :],
                    in_=grouped[part][:, g, h0:h0 + count, :, :].rearrange("p h q j -> p (h q j)"),
                )
                for t in range(2):
                    m0 = g * 256 + t * P
                    nc.tensor.matmul_mx(
                        out=accs[t][:],
                        lhsT=x_codes[:, m0:m0 + P].bitcast(FP8X4),
                        lhsT_scale=x_scales[:, m0:m0 + P],
                        rhs=codes[:, g, :].bitcast(FP8X4),
                        rhs_scale=scales[:, g, :],
                        start=(g == 0),
                        stop=(g == NG - 1),
                    )
            for t in range(2):
                rows = slice(32 * (h0 % 2), 32 * (h0 % 2 + count))
                res = out_sb[2 * (h0 // 2) + t]
                dst = res[:, rows, part * CHUNK:(part + 1) * CHUNK].rearrange("m (h r) q -> m h r q", h=count)
                src = accs[t][:].rearrange("m (h q r) -> m h r q", h=count, q=CHUNK)
                if c == len(chunks) - 1 and t == 1:
                    nc.vector.tensor_copy(out=dst, in_=src)
                else:
                    nc.scalar.copy(out=dst, in_=src)
                if part == 0:
                    nc.sync.dma_start(
                        out=out[t * P:(t + 1) * P, h0 * 512:(h0 + count) * 512],
                        in_=res[:, rows, :].rearrange("m r q -> m (r q)"),
                    )
